import numpy as np
import ml_dtypes


def mxq(x, axis, fmt="e4m3"):
    dtype, down = {"e4m3": (ml_dtypes.float8_e4m3fn, 7), "e5m2": (ml_dtypes.float8_e5m2, 14)}[fmt]
    v = np.moveaxis(np.asarray(x, np.float32).astype(ml_dtypes.bfloat16).astype(np.float64), axis, -1)
    blocks = v.reshape(v.shape[:-1] + (-1, 32))
    amax = np.abs(blocks).max(-1, keepdims=True)
    byte = np.maximum(np.where(amax > 0, np.frexp(amax)[1] - 1 + 127, 0) - down, 1)
    scale = np.exp2(byte - 127.0)
    codes = (blocks / scale).astype(np.float32).astype(dtype).astype(np.float64)
    return np.moveaxis((codes * scale).reshape(v.shape), -1, axis)


WIDE = False


def mx_kscale(k):
    if not WIDE:
        return np.ones(k)
    levels = np.array([10, -10, 5, -5, 0])
    a = np.random.permutation(np.resize(levels, k // 512 * 4)).reshape(k // 512, 4)
    idx = np.arange(k)
    return np.exp2(a[idx // 512, idx % 128 // 32])


BF16 = ml_dtypes.bfloat16


def bf(x):
    return np.asarray(x, np.float32).astype(BF16)


def f64(x):
    return np.asarray(x).astype(np.float64)


B, IM, HID, L = 1024, 1024, 4096, 128


def relu(v):
    return np.maximum(v, 0.0)


def setup_inputs():
    s, t = mx_kscale(IM), mx_kscale(HID)
    return {"x": bf(np.random.random((B, IM)) * s),
            "eps": bf(np.random.standard_normal((B, L))),
            "W11": bf(np.random.standard_normal((IM, HID)) * np.sqrt(3.0 / IM) / s[:, None] * t),
            "b11": bf(np.random.standard_normal(HID) * 0.2 * t),
            "W31": bf(np.random.standard_normal((HID, L)) * np.sqrt(2.0 / HID) / t[:, None]),
            "b31": bf(np.random.standard_normal(L) * 0.2),
            "W32": bf(np.random.standard_normal((HID, L)) * np.sqrt(2.0 / HID) / t[:, None]),
            "b32": bf(np.random.standard_normal(L) * 0.2)}


def reference(x, eps, W11, b11, W31, b31, W32, b32):
    enc = relu((mxq(f64(x), 1, "e4m3") @ mxq(f64(W11), 0, "e4m3")) + f64(b11))
    encq = mxq(enc, 1, "e4m3")
    mu = relu((encq @ mxq(f64(W31), 0, "e4m3")) + f64(b31))
    sigma = relu((encq @ mxq(f64(W32), 0, "e4m3")) + f64(b32))
    z = f64(eps) * sigma + mu
    return mu, sigma, z

@@ -1,0 +1,242 @@
+from contextlib import ExitStack
+
+import concourse.mybir as mybir
+from concourse.masks import make_identity
+
+F32 = mybir.dt.float32
+BF16 = mybir.dt.bfloat16
+U32 = mybir.dt.uint32
+U8 = mybir.dt.uint8
+FP8X4 = mybir.dt.float8_e4m3fn_x4
+RELU = mybir.ActivationFunctionType.Relu
+ADD = mybir.AluOpType.add
+MULT = mybir.AluOpType.mult
+MAX = mybir.AluOpType.max
+
+P = 128
+PACK = 4
+K_PASS = P * PACK
+BATCH = 1024
+IMAGE = 1024
+HIDDEN = 4096
+LATENT = 128
+HALF = 512
+HALVES = BATCH // HALF
+ROW_TILES = BATCH // P
+TILES_PER_HALF = HALF // P
+X_PASSES = IMAGE // K_PASS
+GROUPS = HIDDEN // K_PASS
+RUN = 4
+
+FLOPS = 2 * BATCH * IMAGE * HIDDEN + 2 * 2 * BATCH * HIDDEN * LATENT
+
+
+def regroup(engine_copy, grouped, planes):
+    engine_copy(
+        out=grouped.rearrange("p (a i) t -> p a t i", i=RUN),
+        in_=planes.rearrange("p t (a i) -> p a t i", i=RUN),
+    )
+
+
+def tile_mae_pa_kernel(tc, x, eps, W11, b11, W31, b31, W32, b32, out_0, out_1, out_2):
+    nc = tc.nc
+    with ExitStack() as stack:
+        keep = stack.enter_context(tc.tile_pool(name="keep", bufs=1))
+        stream = stack.enter_context(tc.tile_pool(name="stream", bufs=2))
+        ring = stack.enter_context(tc.psum_pool(name="ring", bufs=4))
+        sums = stack.enter_context(tc.psum_pool(name="sums", bufs=1))
+
+        bias_rows = keep.tile([P, P], BF16)
+        nc.vector.memset(bias_rows[:], 0.0)
+        nc.scalar.dma_start(out=bias_rows[0:32, :], in_=b11.rearrange("(j p) -> j p", p=P))
+        nc.scalar.dma_start(out=bias_rows[32:33, :], in_=b31.rearrange("(j p) -> j p", p=P))
+        nc.scalar.dma_start(out=bias_rows[33:34, :], in_=b32.rearrange("(j p) -> j p", p=P))
+        eps_sb = keep.tile([P, ROW_TILES, LATENT], BF16)
+        nc.scalar.dma_start(out=eps_sb[:], in_=eps.rearrange("(r i) l -> r i l", i=ROW_TILES))
+
+        x_sb = keep.tile([P, ROW_TILES * IMAGE], BF16)
+        x_rows = x.rearrange("(r i) k -> r (i k)", i=ROW_TILES)
+        half_cols = TILES_PER_HALF * IMAGE
+
+        def load_x(h):
+            cols = slice(h * half_cols, (h + 1) * half_cols)
+            nc.sync.dma_start(out=x_sb[:, cols], in_=x_rows[:, cols])
+
+        w11_raw = {}
+
+        def load_w11(g):
+            w11_raw[g] = stream.tile([P, X_PASSES * PACK, K_PASS], BF16, name="w11_raw", bufs=4)
+            for cu in range(X_PASSES * 2):
+                nc.sync.dma_start(
+                    out=w11_raw[g][:, 2 * cu : 2 * cu + 2, :],
+                    in_=W11[256 * cu : 256 * cu + 256, g * K_PASS : (g + 1) * K_PASS].rearrange(
+                        "(q e) w -> q e w", e=2
+                    ),
+                )
+
+        w3_raw = keep.tile([P, GROUPS * PACK, 2 * LATENT], BF16)
+
+        def load_w3():
+            for s, w3 in enumerate((W31, W32)):
+                nc.sync.dma_start(
+                    out=w3_raw[:, :, s * LATENT : (s + 1) * LATENT],
+                    in_=w3.rearrange("(j p) l -> p j l", p=P),
+                )
+
+        load_w11(0)
+        load_x(0)
+        load_w11(1)
+        load_x(1)
+        load_w11(2)
+        load_w3()
+        load_w11(3)
+
+        ident = keep.tile([P, P], F32)
+        make_identity(nc, ident[:])
+
+        bias_rows_f32 = keep.tile([P, P], F32)
+        nc.vector.tensor_copy(out=bias_rows_f32[:], in_=bias_rows[:])
+        bias_bank = ring.tile([P, HALF], F32, name="bank")
+        nc.tensor.transpose(bias_bank[:, 0:P], bias_rows_f32[:], ident[:])
+        bias_cols = keep.tile([P, P], F32)
+        nc.scalar.copy(out=bias_cols[:], in_=bias_bank[:, 0:P])
+
+        x_words = x_sb[:].bitcast(F32)
+        x_codes = keep.tile([P, HALVES * X_PASSES * HALF], U32, align_bytes=64)
+        x_scales = keep.tile([P, HALVES * X_PASSES * HALF], U8, align_bytes=64)
+
+        def prep_x(h):
+            x_grouped = stream.tile([P, X_PASSES * HALF * PACK], BF16, name="x_grouped", align_bytes=64)
+            grouped_words = x_grouped[:].bitcast(F32)
+            for c in range(X_PASSES):
+                for j in range(TILES_PER_HALF // 2):
+                    bank = ring.tile([P, 2, 2, P], F32, name="bank")
+                    for i in range(2):
+                        row_tile = h * TILES_PER_HALF + 2 * j + i
+                        for u in range(2):
+                            first = row_tile * (IMAGE // 2) + c * 256 + u * P
+                            nc.tensor.transpose(bank[:, i, u, :], x_words[:, first : first + P], ident[:])
+                    first = (c * TILES_PER_HALF + 2 * j) * 2 * P
+                    nc.scalar.copy(
+                        out=grouped_words[:, first : first + 4 * P].rearrange("p (i r u) -> p i r u", i=2, u=2),
+                        in_=bank[:].rearrange("p i u r -> p i r u"),
+                    )
+            cols = slice(h * X_PASSES * HALF, (h + 1) * X_PASSES * HALF)
+            nc.vector.quantize_mx(out=x_codes[:, cols].bitcast(FP8X4), scales=x_scales[:, cols], in_=x_grouped[:])
+
+        w11_codes = {}
+        w11_scales = {}
+
+        def prep_w11(g):
+            w11_grouped = stream.tile([P, X_PASSES, K_PASS, PACK], BF16, name="w11_grouped", align_bytes=64)
+            for c in range(X_PASSES):
+                regroup(nc.vector.tensor_copy, w11_grouped[:, c, :, :], w11_raw[g][:, c * PACK : (c + 1) * PACK, :])
+            w11_codes[g] = stream.tile([P, X_PASSES * K_PASS], U32, name="w11_codes", bufs=3, align_bytes=64)
+            w11_scales[g] = stream.tile([P, X_PASSES * K_PASS], U8, name="w11_scales", bufs=3, align_bytes=64)
+            nc.vector.quantize_mx(
+                out=w11_codes[g][:].bitcast(FP8X4),
+                scales=w11_scales[g][:],
+                in_=w11_grouped[:].rearrange("p c w t -> p (c w t)"),
+            )
+
+        w3_codes = keep.tile([P, GROUPS * 2 * LATENT], U32, align_bytes=64)
+        w3_scales = keep.tile([P, GROUPS * 2 * LATENT], U8, align_bytes=64)
+
+        def prep_w3(g):
+            w3_grouped = stream.tile([P, 2 * LATENT, PACK], BF16, name="w3_grouped", align_bytes=64)
+            regroup(nc.scalar.copy, w3_grouped[:], w3_raw[:, g * PACK : (g + 1) * PACK, :])
+            cols = slice(g * 2 * LATENT, (g + 1) * 2 * LATENT)
+            nc.vector.quantize_mx(
+                out=w3_codes[:, cols].bitcast(FP8X4),
+                scales=w3_scales[:, cols],
+                in_=w3_grouped[:].rearrange("p w t -> p (w t)"),
+            )
+
+        acc = {}
+        for s in range(2):
+            for h in range(HALVES):
+                acc[(s, h)] = sums.tile([P, HALF], F32, name="acc%d%d" % (s, h))
+
+        def first_product(g, h):
+            planes = stream.tile([P, PACK, HALF], BF16, name="planes", bufs=3)
+            for t in range(PACK):
+                bank = ring.tile([P, HALF], F32, name="bank")
+                for c in range(X_PASSES):
+                    w_cols = slice(c * K_PASS + t * P, c * K_PASS + (t + 1) * P)
+                    x_cols = slice((h * X_PASSES + c) * HALF, (h * X_PASSES + c + 1) * HALF)
+                    nc.tensor.matmul_mx(
+                        out=bank[:],
+                        lhsT=w11_codes[g][:, w_cols].bitcast(FP8X4),
+                        lhsT_scale=w11_scales[g][:, w_cols],
+                        rhs=x_codes[:, x_cols].bitcast(FP8X4),
+                        rhs_scale=x_scales[:, x_cols],
+                        start=(c == 0),
+                        stop=(c == X_PASSES - 1),
+                    )
+                column = g * PACK + t
+                nc.scalar.activation(
+                    out=planes[:, t, :], in_=bank[:], func=RELU, bias=bias_cols[:, column : column + 1], scale=1.0
+                )
+            enc_grouped = stream.tile([P, HALF, PACK], BF16, name="enc_grouped", bufs=3, align_bytes=64)
+            regroup(nc.vector.tensor_copy, enc_grouped[:], planes[:])
+            enc_codes = stream.tile([P, HALF], U32, name="enc_codes", bufs=6, align_bytes=64)
+            enc_scales = stream.tile([P, HALF], U8, name="enc_scales", bufs=6, align_bytes=64)
+            nc.vector.quantize_mx(
+                out=enc_codes[:].bitcast(FP8X4),
+                scales=enc_scales[:],
+                in_=enc_grouped[:].rearrange("p w t -> p (w t)"),
+            )
+            return enc_codes, enc_scales
+
+        def second_product(g, h, enc_codes, enc_scales):
+            for s in range(2):
+                w_cols = slice((g * 2 + s) * LATENT, (g * 2 + s + 1) * LATENT)
+                nc.tensor.matmul_mx(
+                    out=acc[(s, h)][:],
+                    lhsT=w3_codes[:, w_cols].bitcast(FP8X4),
+                    lhsT_scale=w3_scales[:, w_cols],
+                    rhs=enc_codes[:].bitcast(FP8X4),
+                    rhs_scale=enc_scales[:],
+                    start=(g == 0),
+                    stop=(g == GROUPS - 1),
+                )
+
+        prep_w11(0)
+        prep_x(0)
+        prep_w11(1)
+        prep_x(1)
+        for g in range(GROUPS):
+            if g + 2 < GROUPS:
+                prep_w11(g + 2)
+            if g + 4 < GROUPS:
+                load_w11(g + 4)
+            prep_w3(g)
+            for h in range(HALVES):
+                enc_codes, enc_scales = first_product(g, h)
+                second_product(g, h, enc_codes, enc_scales)
+
+        mu_out = keep.tile([P, ROW_TILES, LATENT], F32)
+        sigma_out = keep.tile([P, ROW_TILES, LATENT], F32)
+        z_out = keep.tile([P, ROW_TILES, LATENT], F32)
+        for h in range(HALVES):
+            tiles = slice(h * TILES_PER_HALF, (h + 1) * TILES_PER_HALF)
+            mu_t = stream.tile([P, HALF], F32, name="mu_t")
+            nc.scalar.activation(out=mu_t[:], in_=acc[(0, h)][:], func=RELU, bias=bias_cols[:, 32:33], scale=1.0)
+            sigma_t = stream.tile([P, HALF], F32, name="sigma_t")
+            nc.vector.tensor_scalar(
+                out=sigma_t[:], in0=acc[(1, h)][:], scalar1=bias_cols[:, 33:34], scalar2=0.0, op0=ADD, op1=MAX
+            )
+            mu_bank = ring.tile([P, TILES_PER_HALF, LATENT], F32, name="bank")
+            sigma_bank = ring.tile([P, TILES_PER_HALF, LATENT], F32, name="bank")
+            for i in range(TILES_PER_HALF):
+                nc.tensor.transpose(mu_bank[:, i, :], mu_t[:, i * P : (i + 1) * P], ident[:])
+            for i in range(TILES_PER_HALF):
+                nc.tensor.transpose(sigma_bank[:, i, :], sigma_t[:, i * P : (i + 1) * P], ident[:])
+            nc.scalar.copy(out=mu_out[:, tiles, :], in_=mu_bank[:])
+            nc.vector.tensor_copy(out=sigma_out[:, tiles, :], in_=sigma_bank[:])
+            nc.vector.tensor_tensor(out=z_out[:, tiles, :], in0=eps_sb[:, tiles, :], in1=sigma_bank[:], op=MULT)
+            nc.vector.tensor_tensor(out=z_out[:, tiles, :], in0=z_out[:, tiles, :], in1=mu_out[:, tiles, :], op=ADD)
+            for result, dram in ((mu_out, out_0), (sigma_out, out_1), (z_out, out_2)):
+                nc.sync.dma_start(
+                    out=dram.rearrange("(r i) l -> r i l", i=ROW_TILES)[:, tiles, :], in_=result[:, tiles, :]
+                )

@@ -26,6 +26,8 @@ ROW_TILES = BATCH // P
 TILES_PER_HALF = HALF // P
 X_PASSES = IMAGE // K_PASS
 GROUPS = HIDDEN // K_PASS
+VECTOR_COLS = 448
+LAG = 4
 RUN = 4
 
 FLOPS = 2 * BATCH * IMAGE * HIDDEN + 2 * 2 * BATCH * HIDDEN * LATENT
@@ -178,7 +180,8 @@ def tile_mae_pa_kernel(tc, x, eps, W11, b11, W31, b31, W32, b32, out_0, out_1, o
                     out=planes[:, t, :], in_=bank[:], func=RELU, bias=bias_cols[:, column : column + 1], scale=1.0
                 )
             enc_grouped = stream.tile([P, HALF, PACK], BF16, name="enc_grouped", bufs=3, align_bytes=64)
-            regroup(nc.vector.tensor_copy, enc_grouped[:], planes[:])
+            regroup(nc.vector.tensor_copy, enc_grouped[:, 0:VECTOR_COLS, :], planes[:, :, 0:VECTOR_COLS])
+            regroup(nc.scalar.copy, enc_grouped[:, VECTOR_COLS:HALF, :], planes[:, :, VECTOR_COLS:HALF])
             enc_codes = stream.tile([P, HALF], U32, name="enc_codes", bufs=6, align_bytes=64)
             enc_scales = stream.tile([P, HALF], U8, name="enc_scales", bufs=6, align_bytes=64)
             nc.vector.quantize_mx(
@@ -201,6 +204,7 @@ def tile_mae_pa_kernel(tc, x, eps, W11, b11, W31, b31, W32, b32, out_0, out_1, o
                     stop=(g == GROUPS - 1),
                 )
 
+        quantised = {}
         prep_w11(0)
         prep_x(0)
         prep_w11(1)
@@ -212,8 +216,12 @@ def tile_mae_pa_kernel(tc, x, eps, W11, b11, W31, b31, W32, b32, out_0, out_1, o
                 load_w11(g + 4)
             prep_w3(g)
             for h in range(HALVES):
-                enc_codes, enc_scales = first_product(g, h)
-                second_product(g, h, enc_codes, enc_scales)
+                quantised[(g, h)] = first_product(g, h)
+                unit = g * HALVES + h - LAG
+                if unit >= 0:
+                    second_product(unit // HALVES, unit % HALVES, *quantised[(unit // HALVES, unit % HALVES)])
+        for unit in range(GROUPS * HALVES - LAG, GROUPS * HALVES):
+            second_product(unit // HALVES, unit % HALVES, *quantised[(unit // HALVES, unit % HALVES)])
 
         mu_out = keep.tile([P, ROW_TILES, LATENT], F32)
         sigma_out = keep.tile([P, ROW_TILES, LATENT], F32)
@@ -226,17 +234,20 @@ def tile_mae_pa_kernel(tc, x, eps, W11, b11, W31, b31, W32, b32, out_0, out_1, o
             nc.vector.tensor_scalar(
                 out=sigma_t[:], in0=acc[(1, h)][:], scalar1=bias_cols[:, 33:34], scalar2=0.0, op0=ADD, op1=MAX
             )
-            mu_bank = ring.tile([P, TILES_PER_HALF, LATENT], F32, name="bank")
             sigma_bank = ring.tile([P, TILES_PER_HALF, LATENT], F32, name="bank")
             for i in range(TILES_PER_HALF):
-                nc.tensor.transpose(mu_bank[:, i, :], mu_t[:, i * P : (i + 1) * P], ident[:])
-            for i in range(TILES_PER_HALF):
                 nc.tensor.transpose(sigma_bank[:, i, :], sigma_t[:, i * P : (i + 1) * P], ident[:])
-            nc.scalar.copy(out=mu_out[:, tiles, :], in_=mu_bank[:])
-            nc.vector.tensor_copy(out=sigma_out[:, tiles, :], in_=sigma_bank[:])
+            mu_bank = ring.tile([P, TILES_PER_HALF, LATENT], F32, name="bank")
+            for i in range(TILES_PER_HALF):
+                nc.tensor.transpose(mu_bank[:, i, :], mu_t[:, i * P : (i + 1) * P], ident[:])
+            sigma_bank_2 = ring.tile([P, TILES_PER_HALF, LATENT], F32, name="bank")
+            for i in range(TILES_PER_HALF):
+                nc.tensor.transpose(sigma_bank_2[:, i, :], sigma_t[:, i * P : (i + 1) * P], ident[:])
             nc.vector.tensor_tensor(out=z_out[:, tiles, :], in0=eps_sb[:, tiles, :], in1=sigma_bank[:], op=MULT)
+            nc.scalar.copy(out=mu_out[:, tiles, :], in_=mu_bank[:])
             nc.vector.tensor_tensor(out=z_out[:, tiles, :], in0=z_out[:, tiles, :], in1=mu_out[:, tiles, :], op=ADD)
-            for result, dram in ((mu_out, out_0), (sigma_out, out_1), (z_out, out_2)):
+            nc.scalar.copy(out=sigma_out[:, tiles, :], in_=sigma_bank_2[:])
+            for result, dram in ((mu_out, out_0), (z_out, out_2), (sigma_out, out_1)):
                 nc.sync.dma_start(
                     out=dram.rearrange("(r i) l -> r i l", i=ROW_TILES)[:, tiles, :], in_=result[:, tiles, :]
                 )

@@ -78,11 +78,11 @@ def tile_mae_pa_kernel(tc, x, eps, W11, b11, W31, b31, W32, b32, out_0, out_1, o
 
         w3_raw = keep.tile([P, GROUPS * PACK, 2 * LATENT], BF16)
 
-        def load_w3():
+        def load_w3(g):
             for s, w3 in enumerate((W31, W32)):
                 nc.sync.dma_start(
-                    out=w3_raw[:, :, s * LATENT : (s + 1) * LATENT],
-                    in_=w3.rearrange("(j p) l -> p j l", p=P),
+                    out=w3_raw[:, g * PACK : (g + 1) * PACK, s * LATENT : (s + 1) * LATENT],
+                    in_=w3[g * K_PASS : (g + 1) * K_PASS, :].rearrange("(t p) l -> p t l", p=P),
                 )
 
         load_w11(0)
@@ -90,7 +90,8 @@ def tile_mae_pa_kernel(tc, x, eps, W11, b11, W31, b31, W32, b32, out_0, out_1, o
         load_w11(1)
         load_x(1)
         load_w11(2)
-        load_w3()
+        load_w3(0)
+        load_w3(1)
         load_w11(3)
 
         ident = keep.tile([P, P], F32)
@@ -214,6 +215,8 @@ def tile_mae_pa_kernel(tc, x, eps, W11, b11, W31, b31, W32, b32, out_0, out_1, o
                 prep_w11(g + 2)
             if g + 4 < GROUPS:
                 load_w11(g + 4)
+            if g + 2 < GROUPS:
+                load_w3(g + 2)
             prep_w3(g)
             for h in range(HALVES):
                 quantised[(g, h)] = first_product(g, h)

@@ -26,7 +26,7 @@ ROW_TILES = BATCH // P
 TILES_PER_HALF = HALF // P
 X_PASSES = IMAGE // K_PASS
 GROUPS = HIDDEN // K_PASS
-VECTOR_COLS = 448
+VECTOR_COLS = 464
 LAG = 4
 RUN = 4
 
@@ -61,8 +61,10 @@ def tile_mae_pa_kernel(tc, x, eps, W11, b11, W31, b31, W32, b32, out_0, out_1, o
         half_cols = TILES_PER_HALF * IMAGE
 
         def load_x(h):
-            cols = slice(h * half_cols, (h + 1) * half_cols)
-            nc.sync.dma_start(out=x_sb[:, cols], in_=x_rows[:, cols])
+            for j in range(TILES_PER_HALF // 2):
+                first = h * half_cols + j * 2 * IMAGE
+                cols = slice(first, first + 2 * IMAGE)
+                nc.sync.dma_start(out=x_sb[:, cols], in_=x_rows[:, cols])
 
         w11_raw = {}
 
@@ -111,8 +113,8 @@ def tile_mae_pa_kernel(tc, x, eps, W11, b11, W31, b31, W32, b32, out_0, out_1, o
         def prep_x(h):
             x_grouped = stream.tile([P, X_PASSES * HALF * PACK], BF16, name="x_grouped", align_bytes=64)
             grouped_words = x_grouped[:].bitcast(F32)
-            for c in range(X_PASSES):
-                for j in range(TILES_PER_HALF // 2):
+            for j in range(TILES_PER_HALF // 2):
+                for c in range(X_PASSES):
                     bank = ring.tile([P, 2, 2, P], F32, name="bank")
                     for i in range(2):
                         row_tile = h * TILES_PER_HALF + 2 * j + i
@@ -160,15 +162,16 @@ def tile_mae_pa_kernel(tc, x, eps, W11, b11, W31, b31, W32, b32, out_0, out_1, o
             for h in range(HALVES):
                 acc[(s, h)] = sums.tile([P, HALF], F32, name="acc%d%d" % (s, h))
 
-        def first_product(g, h):
+        def first_product(g, h, begin, width, enc_codes, enc_scales):
             planes = stream.tile([P, PACK, HALF], BF16, name="planes", bufs=3)
             for t in range(PACK):
                 bank = ring.tile([P, HALF], F32, name="bank")
                 for c in range(X_PASSES):
                     w_cols = slice(c * K_PASS + t * P, c * K_PASS + (t + 1) * P)
-                    x_cols = slice((h * X_PASSES + c) * HALF, (h * X_PASSES + c + 1) * HALF)
+                    first = (h * X_PASSES + c) * HALF + begin
+                    x_cols = slice(first, first + width)
                     nc.tensor.matmul_mx(
-                        out=bank[:],
+                        out=bank[:, 0:width],
                         lhsT=w11_codes[g][:, w_cols].bitcast(FP8X4),
                         lhsT_scale=w11_scales[g][:, w_cols],
                         rhs=x_codes[:, x_cols].bitcast(FP8X4),
@@ -178,34 +181,43 @@ def tile_mae_pa_kernel(tc, x, eps, W11, b11, W31, b31, W32, b32, out_0, out_1, o
                     )
                 column = g * PACK + t
                 nc.scalar.activation(
-                    out=planes[:, t, :], in_=bank[:], func=RELU, bias=bias_cols[:, column : column + 1], scale=1.0
+                    out=planes[:, t, 0:width], in_=bank[:, 0:width], func=RELU, bias=bias_cols[:, column : column + 1], scale=1.0
                 )
             enc_grouped = stream.tile([P, HALF, PACK], BF16, name="enc_grouped", bufs=3, align_bytes=64)
-            regroup(nc.vector.tensor_copy, enc_grouped[:, 0:VECTOR_COLS, :], planes[:, :, 0:VECTOR_COLS])
-            regroup(nc.scalar.copy, enc_grouped[:, VECTOR_COLS:HALF, :], planes[:, :, VECTOR_COLS:HALF])
-            enc_codes = stream.tile([P, HALF], U32, name="enc_codes", bufs=6, align_bytes=64)
-            enc_scales = stream.tile([P, HALF], U8, name="enc_scales", bufs=6, align_bytes=64)
+            split = VECTOR_COLS * width // HALF
+            regroup(nc.vector.tensor_copy, enc_grouped[:, 0:split, :], planes[:, :, 0:split])
+            regroup(nc.scalar.copy, enc_grouped[:, split:width, :], planes[:, :, split:width])
+            cols = slice(begin, begin + width)
             nc.vector.quantize_mx(
-                out=enc_codes[:].bitcast(FP8X4),
-                scales=enc_scales[:],
-                in_=enc_grouped[:].rearrange("p w t -> p (w t)"),
+                out=enc_codes[:, cols].bitcast(FP8X4),
+                scales=enc_scales[:, cols],
+                in_=enc_grouped[:, 0:width, :].rearrange("p w t -> p (w t)"),
             )
-            return enc_codes, enc_scales
 
-        def second_product(g, h, enc_codes, enc_scales):
-            for s in range(2):
+        def second_product(g, h, begin, width, enc_codes, enc_scales):
+            cols = slice(begin, begin + width)
+            for s in (1, 0):
                 w_cols = slice((g * 2 + s) * LATENT, (g * 2 + s + 1) * LATENT)
                 nc.tensor.matmul_mx(
-                    out=acc[(s, h)][:],
+                    out=acc[(s, h)][:, cols],
                     lhsT=w3_codes[:, w_cols].bitcast(FP8X4),
                     lhsT_scale=w3_scales[:, w_cols],
-                    rhs=enc_codes[:].bitcast(FP8X4),
-                    rhs_scale=enc_scales[:],
+                    rhs=enc_codes[:, cols].bitcast(FP8X4),
+                    rhs_scale=enc_scales[:, cols],
                     start=(g == 0),
-                    stop=(g == GROUPS - 1),
+                    stop=(g == GROUPS - 1 and begin + width == HALF),
                 )
 
         quantised = {}
+
+        def pieces(unit):
+            width = HALF // 2 if unit == GROUPS * HALVES - 1 else HALF
+            return [(begin, width) for begin in range(0, HALF, width)]
+
+        def second_unit(unit):
+            for begin, width in pieces(unit):
+                second_product(unit // HALVES, unit % HALVES, begin, width, *quantised[unit])
+
         prep_w11(0)
         prep_x(0)
         prep_w11(1)
@@ -219,12 +231,16 @@ def tile_mae_pa_kernel(tc, x, eps, W11, b11, W31, b31, W32, b32, out_0, out_1, o
                 load_w3(g + 2)
             prep_w3(g)
             for h in range(HALVES):
-                quantised[(g, h)] = first_product(g, h)
-                unit = g * HALVES + h - LAG
-                if unit >= 0:
-                    second_product(unit // HALVES, unit % HALVES, *quantised[(unit // HALVES, unit % HALVES)])
+                unit = g * HALVES + h
+                enc_codes = stream.tile([P, HALF], U32, name="enc_codes", bufs=6, align_bytes=64)
+                enc_scales = stream.tile([P, HALF], U8, name="enc_scales", bufs=6, align_bytes=64)
+                quantised[unit] = (enc_codes, enc_scales)
+                for begin, width in pieces(unit):
+                    first_product(g, h, begin, width, enc_codes, enc_scales)
+                if unit >= LAG:
+                    second_unit(unit - LAG)
         for unit in range(GROUPS * HALVES - LAG, GROUPS * HALVES):
-            second_product(unit // HALVES, unit % HALVES, *quantised[(unit // HALVES, unit % HALVES)])
+            second_unit(unit)
 
         mu_out = keep.tile([P, ROW_TILES, LATENT], F32)
         sigma_out = keep.tile([P, ROW_TILES, LATENT], F32)

from contextlib import ExitStack

import concourse.mybir as mybir
from concourse.masks import make_identity

F32 = mybir.dt.float32
BF16 = mybir.dt.bfloat16
U32 = mybir.dt.uint32
U8 = mybir.dt.uint8
FP8X4 = mybir.dt.float8_e4m3fn_x4
RELU = mybir.ActivationFunctionType.Relu
ADD = mybir.AluOpType.add
MULT = mybir.AluOpType.mult
MAX = mybir.AluOpType.max

P = 128
PACK = 4
K_PASS = P * PACK
BATCH = 1024
IMAGE = 1024
HIDDEN = 4096
LATENT = 128
HALF = 512
HALVES = BATCH // HALF
ROW_TILES = BATCH // P
TILES_PER_HALF = HALF // P
X_PASSES = IMAGE // K_PASS
GROUPS = HIDDEN // K_PASS
VECTOR_COLS = 464
LAG = 4
RUN = 4

FLOPS = 2 * BATCH * IMAGE * HIDDEN + 2 * 2 * BATCH * HIDDEN * LATENT


def regroup(engine_copy, grouped, planes):
    engine_copy(
        out=grouped.rearrange("p (a i) t -> p a t i", i=RUN),
        in_=planes.rearrange("p t (a i) -> p a t i", i=RUN),
    )


def tile_mae_pa_kernel(tc, x, eps, W11, b11, W31, b31, W32, b32, out_0, out_1, out_2):
    nc = tc.nc
    with ExitStack() as stack:
        keep = stack.enter_context(tc.tile_pool(name="keep", bufs=1))
        stream = stack.enter_context(tc.tile_pool(name="stream", bufs=2))
        ring = stack.enter_context(tc.psum_pool(name="ring", bufs=4))
        sums = stack.enter_context(tc.psum_pool(name="sums", bufs=1))

        bias_rows = keep.tile([P, P], BF16)
        nc.vector.memset(bias_rows[:], 0.0)
        nc.scalar.dma_start(out=bias_rows[0:32, :], in_=b11.rearrange("(j p) -> j p", p=P))
        nc.scalar.dma_start(out=bias_rows[32:33, :], in_=b31.rearrange("(j p) -> j p", p=P))
        nc.scalar.dma_start(out=bias_rows[33:34, :], in_=b32.rearrange("(j p) -> j p", p=P))
        eps_sb = keep.tile([P, ROW_TILES, LATENT], BF16)
        nc.scalar.dma_start(out=eps_sb[:], in_=eps.rearrange("(r i) l -> r i l", i=ROW_TILES))

        x_sb = keep.tile([P, ROW_TILES * IMAGE], BF16)
        x_rows = x.rearrange("(r i) k -> r (i k)", i=ROW_TILES)
        half_cols = TILES_PER_HALF * IMAGE

        def load_x(h):
            for j in range(TILES_PER_HALF // 2):
                first = h * half_cols + j * 2 * IMAGE
                cols = slice(first, first + 2 * IMAGE)
                nc.sync.dma_start(out=x_sb[:, cols], in_=x_rows[:, cols])

        w11_raw = {}

        def load_w11(g):
            w11_raw[g] = stream.tile([P, X_PASSES * PACK, K_PASS], BF16, name="w11_raw", bufs=4)
            for cu in range(X_PASSES * 2):
                nc.sync.dma_start(
                    out=w11_raw[g][:, 2 * cu : 2 * cu + 2, :],
                    in_=W11[256 * cu : 256 * cu + 256, g * K_PASS : (g + 1) * K_PASS].rearrange(
                        "(q e) w -> q e w", e=2
                    ),
                )

        w3_raw = keep.tile([P, GROUPS * PACK, 2 * LATENT], BF16)

        def load_w3(g):
            for s, w3 in enumerate((W31, W32)):
                nc.sync.dma_start(
                    out=w3_raw[:, g * PACK : (g + 1) * PACK, s * LATENT : (s + 1) * LATENT],
                    in_=w3[g * K_PASS : (g + 1) * K_PASS, :].rearrange("(t p) l -> p t l", p=P),
                )

        load_w11(0)
        load_x(0)
        load_w11(1)
        load_x(1)
        load_w11(2)
        load_w3(0)
        load_w3(1)
        load_w11(3)

        ident = keep.tile([P, P], F32)
        make_identity(nc, ident[:])

        bias_rows_f32 = keep.tile([P, P], F32)
        nc.vector.tensor_copy(out=bias_rows_f32[:], in_=bias_rows[:])
        bias_bank = ring.tile([P, HALF], F32, name="bank")
        nc.tensor.transpose(bias_bank[:, 0:P], bias_rows_f32[:], ident[:])
        bias_cols = keep.tile([P, P], F32)
        nc.scalar.copy(out=bias_cols[:], in_=bias_bank[:, 0:P])

        x_words = x_sb[:].bitcast(F32)
        x_codes = keep.tile([P, HALVES * X_PASSES * HALF], U32, align_bytes=64)
        x_scales = keep.tile([P, HALVES * X_PASSES * HALF], U8, align_bytes=64)

        def prep_x(h):
            x_grouped = stream.tile([P, X_PASSES * HALF * PACK], BF16, name="x_grouped", align_bytes=64)
            grouped_words = x_grouped[:].bitcast(F32)
            for j in range(TILES_PER_HALF // 2):
                for c in range(X_PASSES):
                    bank = ring.tile([P, 2, 2, P], F32, name="bank")
                    for i in range(2):
                        row_tile = h * TILES_PER_HALF + 2 * j + i
                        for u in range(2):
                            first = row_tile * (IMAGE // 2) + c * 256 + u * P
                            nc.tensor.transpose(bank[:, i, u, :], x_words[:, first : first + P], ident[:])
                    first = (c * TILES_PER_HALF + 2 * j) * 2 * P
                    nc.scalar.copy(
                        out=grouped_words[:, first : first + 4 * P].rearrange("p (i r u) -> p i r u", i=2, u=2),
                        in_=bank[:].rearrange("p i u r -> p i r u"),
                    )
            cols = slice(h * X_PASSES * HALF, (h + 1) * X_PASSES * HALF)
            nc.vector.quantize_mx(out=x_codes[:, cols].bitcast(FP8X4), scales=x_scales[:, cols], in_=x_grouped[:])

        w11_codes = {}
        w11_scales = {}

        def prep_w11(g):
            w11_grouped = stream.tile([P, X_PASSES, K_PASS, PACK], BF16, name="w11_grouped", align_bytes=64)
            for c in range(X_PASSES):
                regroup(nc.vector.tensor_copy, w11_grouped[:, c, :, :], w11_raw[g][:, c * PACK : (c + 1) * PACK, :])
            w11_codes[g] = stream.tile([P, X_PASSES * K_PASS], U32, name="w11_codes", bufs=3, align_bytes=64)
            w11_scales[g] = stream.tile([P, X_PASSES * K_PASS], U8, name="w11_scales", bufs=3, align_bytes=64)
            nc.vector.quantize_mx(
                out=w11_codes[g][:].bitcast(FP8X4),
                scales=w11_scales[g][:],
                in_=w11_grouped[:].rearrange("p c w t -> p (c w t)"),
            )

        w3_codes = keep.tile([P, GROUPS * 2 * LATENT], U32, align_bytes=64)
        w3_scales = keep.tile([P, GROUPS * 2 * LATENT], U8, align_bytes=64)

        def prep_w3(g):
            w3_grouped = stream.tile([P, 2 * LATENT, PACK], BF16, name="w3_grouped", align_bytes=64)
            regroup(nc.scalar.copy, w3_grouped[:], w3_raw[:, g * PACK : (g + 1) * PACK, :])
            cols = slice(g * 2 * LATENT, (g + 1) * 2 * LATENT)
            nc.vector.quantize_mx(
                out=w3_codes[:, cols].bitcast(FP8X4),
                scales=w3_scales[:, cols],
                in_=w3_grouped[:].rearrange("p w t -> p (w t)"),
            )

        acc = {}
        for s in range(2):
            for h in range(HALVES):
                acc[(s, h)] = sums.tile([P, HALF], F32, name="acc%d%d" % (s, h))

        def first_product(g, h, begin, width, enc_codes, enc_scales):
            planes = stream.tile([P, PACK, HALF], BF16, name="planes", bufs=3)
            for t in range(PACK):
                bank = ring.tile([P, HALF], F32, name="bank")
                for c in range(X_PASSES):
                    w_cols = slice(c * K_PASS + t * P, c * K_PASS + (t + 1) * P)
                    first = (h * X_PASSES + c) * HALF + begin
                    x_cols = slice(first, first + width)
                    nc.tensor.matmul_mx(
                        out=bank[:, 0:width],
                        lhsT=w11_codes[g][:, w_cols].bitcast(FP8X4),
                        lhsT_scale=w11_scales[g][:, w_cols],
                        rhs=x_codes[:, x_cols].bitcast(FP8X4),
                        rhs_scale=x_scales[:, x_cols],
                        start=(c == 0),
                        stop=(c == X_PASSES - 1),
                    )
                column = g * PACK + t
                nc.scalar.activation(
                    out=planes[:, t, 0:width], in_=bank[:, 0:width], func=RELU, bias=bias_cols[:, column : column + 1], scale=1.0
                )
            enc_grouped = stream.tile([P, HALF, PACK], BF16, name="enc_grouped", bufs=3, align_bytes=64)
            split = VECTOR_COLS * width // HALF
            regroup(nc.vector.tensor_copy, enc_grouped[:, 0:split, :], planes[:, :, 0:split])
            regroup(nc.scalar.copy, enc_grouped[:, split:width, :], planes[:, :, split:width])
            cols = slice(begin, begin + width)
            nc.vector.quantize_mx(
                out=enc_codes[:, cols].bitcast(FP8X4),
                scales=enc_scales[:, cols],
                in_=enc_grouped[:, 0:width, :].rearrange("p w t -> p (w t)"),
            )

        def second_product(g, h, begin, width, enc_codes, enc_scales):
            cols = slice(begin, begin + width)
            for s in (1, 0):
                w_cols = slice((g * 2 + s) * LATENT, (g * 2 + s + 1) * LATENT)
                nc.tensor.matmul_mx(
                    out=acc[(s, h)][:, cols],
                    lhsT=w3_codes[:, w_cols].bitcast(FP8X4),
                    lhsT_scale=w3_scales[:, w_cols],
                    rhs=enc_codes[:, cols].bitcast(FP8X4),
                    rhs_scale=enc_scales[:, cols],
                    start=(g == 0),
                    stop=(g == GROUPS - 1 and begin + width == HALF),
                )

        quantised = {}

        def pieces(unit):
            width = HALF // 2 if unit == GROUPS * HALVES - 1 else HALF
            return [(begin, width) for begin in range(0, HALF, width)]

        def second_unit(unit):
            for begin, width in pieces(unit):
                second_product(unit // HALVES, unit % HALVES, begin, width, *quantised[unit])

        prep_w11(0)
        prep_x(0)
        prep_w11(1)
        prep_x(1)
        for g in range(GROUPS):
            if g + 2 < GROUPS:
                prep_w11(g + 2)
            if g + 4 < GROUPS:
                load_w11(g + 4)
            if g + 2 < GROUPS:
                load_w3(g + 2)
            prep_w3(g)
            for h in range(HALVES):
                unit = g * HALVES + h
                enc_codes = stream.tile([P, HALF], U32, name="enc_codes", bufs=6, align_bytes=64)
                enc_scales = stream.tile([P, HALF], U8, name="enc_scales", bufs=6, align_bytes=64)
                quantised[unit] = (enc_codes, enc_scales)
                for begin, width in pieces(unit):
                    first_product(g, h, begin, width, enc_codes, enc_scales)
                if unit >= LAG:
                    second_unit(unit - LAG)
        for unit in range(GROUPS * HALVES - LAG, GROUPS * HALVES):
            second_unit(unit)

        mu_out = keep.tile([P, ROW_TILES, LATENT], F32)
        sigma_out = keep.tile([P, ROW_TILES, LATENT], F32)
        z_out = keep.tile([P, ROW_TILES, LATENT], F32)
        for h in range(HALVES):
            tiles = slice(h * TILES_PER_HALF, (h + 1) * TILES_PER_HALF)
            mu_t = stream.tile([P, HALF], F32, name="mu_t")
            nc.scalar.activation(out=mu_t[:], in_=acc[(0, h)][:], func=RELU, bias=bias_cols[:, 32:33], scale=1.0)
            sigma_t = stream.tile([P, HALF], F32, name="sigma_t")
            nc.vector.tensor_scalar(
                out=sigma_t[:], in0=acc[(1, h)][:], scalar1=bias_cols[:, 33:34], scalar2=0.0, op0=ADD, op1=MAX
            )
            sigma_bank = ring.tile([P, TILES_PER_HALF, LATENT], F32, name="bank")
            for i in range(TILES_PER_HALF):
                nc.tensor.transpose(sigma_bank[:, i, :], sigma_t[:, i * P : (i + 1) * P], ident[:])
            mu_bank = ring.tile([P, TILES_PER_HALF, LATENT], F32, name="bank")
            for i in range(TILES_PER_HALF):
                nc.tensor.transpose(mu_bank[:, i, :], mu_t[:, i * P : (i + 1) * P], ident[:])
            sigma_bank_2 = ring.tile([P, TILES_PER_HALF, LATENT], F32, name="bank")
            for i in range(TILES_PER_HALF):
                nc.tensor.transpose(sigma_bank_2[:, i, :], sigma_t[:, i * P : (i + 1) * P], ident[:])
            nc.vector.tensor_tensor(out=z_out[:, tiles, :], in0=eps_sb[:, tiles, :], in1=sigma_bank[:], op=MULT)
            nc.scalar.copy(out=mu_out[:, tiles, :], in_=mu_bank[:])
            nc.vector.tensor_tensor(out=z_out[:, tiles, :], in0=z_out[:, tiles, :], in1=mu_out[:, tiles, :], op=ADD)
            nc.scalar.copy(out=sigma_out[:, tiles, :], in_=sigma_bank_2[:])
            for result, dram in ((mu_out, out_0), (z_out, out_2), (sigma_out, out_1)):
                nc.sync.dma_start(
                    out=dram.rearrange("(r i) l -> r i l", i=ROW_TILES)[:, tiles, :], in_=result[:, tiles, :]
                )
